import numpy as np
import ml_dtypes

BF16 = ml_dtypes.bfloat16


def bf(x):
    return np.asarray(x, np.float32).astype(BF16)


def f32(x):
    return np.asarray(x, np.float32)


def f64(x):
    return np.asarray(x).astype(np.float64)


def striped(idx):
    return np.tile(idx.reshape(-1, 16).T, (8, 1))


D, S, M, K, T, N = 128, 256, 256, 4, 256, 1024
W_SCALE = 0.05
B_SCALE = 0.1


def setup_inputs():
    return {"table": bf(np.random.standard_normal((D, S))), "w": bf(W_SCALE * np.random.standard_normal((D, K * M))), "b": f32(B_SCALE * np.random.standard_normal((M, 1))), "offs": striped(np.concatenate([np.random.permutation(S) for _ in range(K)]))}


def reference(table, w, b, offs):
    idx = offs[:16].T.reshape(-1)
    acc = np.zeros((M, T)) + f64(b)
    for k in range(K):
        acc = acc + f64(w)[:, k * M:(k + 1) * M].T @ f64(table)[:, idx[k * T:(k + 1) * T]]
    return acc

@@ -1,0 +1,52 @@
+import concourse.mybir as mybir
+
+BF16, F32, U16 = mybir.dt.bfloat16, mybir.dt.float32, mybir.dt.uint16
+
+P = 128
+SYMBOLS = 256
+SLOTS = 4
+CONTEXTS = 256
+PIECE = 128
+PER_COLUMN = 16
+
+FLOPS = 2 * P * SLOTS * SYMBOLS * CONTEXTS
+
+
+def tile_representationngramestimator_kernel(tc, table, w, b, offs, out):
+    nc = tc.nc
+    with (
+        tc.tile_pool(name="held", bufs=1) as held,
+        tc.tile_pool(name="staging", bufs=4) as staging,
+        tc.psum_pool(name="psum", bufs=4) as psum,
+    ):
+        offsets = held.tile([P, SLOTS * CONTEXTS // PER_COLUMN], U16, name="offsets")
+        nc.sync.dma_start(offsets[:], offs)
+        embeddings = held.tile([P, SYMBOLS], BF16, name="embeddings")
+        nc.scalar.dma_start(embeddings[:], table)
+        weights = held.tile([P, SLOTS * SYMBOLS], BF16, name="weights")
+        nc.sync.dma_start(weights[:], w)
+        biases = []
+        for block in range(SYMBOLS // P):
+            bias = held.tile([P, 1], F32, name=f"bias{block}")
+            nc.scalar.dma_start(bias[:], b[block * P : (block + 1) * P, :])
+            biases.append(bias)
+
+        for block in range(SYMBOLS // P):
+            for piece in range(CONTEXTS // PIECE):
+                scores = psum.tile([P, PIECE], F32, name="scores")
+                for slot in range(SLOTS):
+                    first = (slot * CONTEXTS + piece * PIECE) // PER_COLUMN
+                    nc.tensor.matmul(
+                        scores[:],
+                        weights[:, slot * SYMBOLS + block * P : slot * SYMBOLS + (block + 1) * P],
+                        embeddings[:].indirect(offsets[:, first : first + PIECE // PER_COLUMN]),
+                        start=(slot == 0),
+                        stop=(slot == SLOTS - 1),
+                    )
+                biased = staging.tile([P, PIECE], F32, name="biased")
+                nc.vector.tensor_scalar(
+                    biased[:], scores[:], biases[block][:, 0:1], None, mybir.AluOpType.add
+                )
+                nc.sync.dma_start(
+                    out[block * P : (block + 1) * P, piece * PIECE : (piece + 1) * PIECE], biased[:]
+                )

@@ -8,6 +8,8 @@ SLOTS = 4
 CONTEXTS = 256
 PIECE = 128
 PER_COLUMN = 16
+BANK = 512
+WARM_UPS = 6
 
 FLOPS = 2 * P * SLOTS * SYMBOLS * CONTEXTS
 
@@ -18,6 +20,7 @@ def tile_representationngramestimator_kernel(tc, table, w, b, offs, out):
         tc.tile_pool(name="held", bufs=1) as held,
         tc.tile_pool(name="staging", bufs=4) as staging,
         tc.psum_pool(name="psum", bufs=4) as psum,
+        tc.psum_pool(name="unread", bufs=1) as unread,
     ):
         offsets = held.tile([P, SLOTS * CONTEXTS // PER_COLUMN], U16, name="offsets")
         nc.sync.dma_start(offsets[:], offs)
@@ -30,6 +33,12 @@ def tile_representationngramestimator_kernel(tc, table, w, b, offs, out):
             bias = held.tile([P, 1], F32, name=f"bias{block}")
             nc.scalar.dma_start(bias[:], b[block * P : (block + 1) * P, :])
             biases.append(bias)
+
+        zeros = held.tile([P, BANK], BF16, name="zeros")
+        nc.vector.memset(zeros[:], 0.0)
+        discarded = unread.tile([P, BANK], F32, name="discarded")
+        for warm_up in range(WARM_UPS):
+            nc.tensor.matmul(discarded[:], zeros[:, 0:P], zeros[:], start=True, stop=True)
 
         for block in range(SYMBOLS // P):
             for piece in range(CONTEXTS // PIECE):

@@ -8,8 +8,6 @@ SLOTS = 4
 CONTEXTS = 256
 PIECE = 128
 PER_COLUMN = 16
-BANK = 512
-WARM_UPS = 6
 
 FLOPS = 2 * P * SLOTS * SYMBOLS * CONTEXTS
 
@@ -20,25 +18,22 @@ def tile_representationngramestimator_kernel(tc, table, w, b, offs, out):
         tc.tile_pool(name="held", bufs=1) as held,
         tc.tile_pool(name="staging", bufs=4) as staging,
         tc.psum_pool(name="psum", bufs=4) as psum,
-        tc.psum_pool(name="unread", bufs=1) as unread,
     ):
         offsets = held.tile([P, SLOTS * CONTEXTS // PER_COLUMN], U16, name="offsets")
         nc.sync.dma_start(offsets[:], offs)
         embeddings = held.tile([P, SYMBOLS], BF16, name="embeddings")
         nc.scalar.dma_start(embeddings[:], table)
-        weights = held.tile([P, SLOTS * SYMBOLS], BF16, name="weights")
-        nc.sync.dma_start(weights[:], w)
+        weights = []
+        for slot in range(SLOTS):
+            slot_weights = held.tile([P, SYMBOLS], BF16, name=f"weights{slot}")
+            queue = nc.sync if slot % 2 == 0 else nc.scalar
+            queue.dma_start(slot_weights[:], w[:, slot * SYMBOLS : (slot + 1) * SYMBOLS])
+            weights.append(slot_weights)
         biases = []
         for block in range(SYMBOLS // P):
             bias = held.tile([P, 1], F32, name=f"bias{block}")
             nc.scalar.dma_start(bias[:], b[block * P : (block + 1) * P, :])
             biases.append(bias)
-
-        zeros = held.tile([P, BANK], BF16, name="zeros")
-        nc.vector.memset(zeros[:], 0.0)
-        discarded = unread.tile([P, BANK], F32, name="discarded")
-        for warm_up in range(WARM_UPS):
-            nc.tensor.matmul(discarded[:], zeros[:, 0:P], zeros[:], start=True, stop=True)
 
         for block in range(SYMBOLS // P):
             for piece in range(CONTEXTS // PIECE):
@@ -47,7 +42,7 @@ def tile_representationngramestimator_kernel(tc, table, w, b, offs, out):
                     first = (slot * CONTEXTS + piece * PIECE) // PER_COLUMN
                     nc.tensor.matmul(
                         scores[:],
-                        weights[:, slot * SYMBOLS + block * P : slot * SYMBOLS + (block + 1) * P],
+                        weights[slot][:, block * P : (block + 1) * P],
                         embeddings[:].indirect(offsets[:, first : first + PIECE // PER_COLUMN]),
                         start=(slot == 0),
                         stop=(slot == SLOTS - 1),

@@ -8,6 +8,7 @@ SLOTS = 4
 CONTEXTS = 256
 PIECE = 128
 PER_COLUMN = 16
+WARM_UPS = 6
 
 FLOPS = 2 * P * SLOTS * SYMBOLS * CONTEXTS
 
@@ -18,6 +19,7 @@ def tile_representationngramestimator_kernel(tc, table, w, b, offs, out):
         tc.tile_pool(name="held", bufs=1) as held,
         tc.tile_pool(name="staging", bufs=4) as staging,
         tc.psum_pool(name="psum", bufs=4) as psum,
+        tc.psum_pool(name="unread", bufs=1) as unread,
     ):
         offsets = held.tile([P, SLOTS * CONTEXTS // PER_COLUMN], U16, name="offsets")
         nc.sync.dma_start(offsets[:], offs)
@@ -34,6 +36,12 @@ def tile_representationngramestimator_kernel(tc, table, w, b, offs, out):
             bias = held.tile([P, 1], F32, name=f"bias{block}")
             nc.scalar.dma_start(bias[:], b[block * P : (block + 1) * P, :])
             biases.append(bias)
+
+        zeros = held.tile([P, CONTEXTS], BF16, name="zeros")
+        nc.gpsimd.memset(zeros[:], 0.0)
+        discarded = unread.tile([P, CONTEXTS], F32, name="discarded")
+        for warm_up in range(WARM_UPS):
+            nc.tensor.matmul(discarded[:], zeros[:, 0:P], zeros[:], start=True, stop=True)
 
         for block in range(SYMBOLS // P):
             for piece in range(CONTEXTS // PIECE):

@@ -8,7 +8,6 @@ SLOTS = 4
 CONTEXTS = 256
 PIECE = 128
 PER_COLUMN = 16
-WARM_UPS = 6
 
 FLOPS = 2 * P * SLOTS * SYMBOLS * CONTEXTS
 
@@ -19,7 +18,6 @@ def tile_representationngramestimator_kernel(tc, table, w, b, offs, out):
         tc.tile_pool(name="held", bufs=1) as held,
         tc.tile_pool(name="staging", bufs=4) as staging,
         tc.psum_pool(name="psum", bufs=4) as psum,
-        tc.psum_pool(name="unread", bufs=1) as unread,
     ):
         offsets = held.tile([P, SLOTS * CONTEXTS // PER_COLUMN], U16, name="offsets")
         nc.sync.dma_start(offsets[:], offs)
@@ -37,12 +35,6 @@ def tile_representationngramestimator_kernel(tc, table, w, b, offs, out):
             nc.scalar.dma_start(bias[:], b[block * P : (block + 1) * P, :])
             biases.append(bias)
 
-        zeros = held.tile([P, CONTEXTS], BF16, name="zeros")
-        nc.gpsimd.memset(zeros[:], 0.0)
-        discarded = unread.tile([P, CONTEXTS], F32, name="discarded")
-        for warm_up in range(WARM_UPS):
-            nc.tensor.matmul(discarded[:], zeros[:, 0:P], zeros[:], start=True, stop=True)
-
         for block in range(SYMBOLS // P):
             for piece in range(CONTEXTS // PIECE):
                 scores = psum.tile([P, PIECE], F32, name="scores")
@@ -56,9 +48,14 @@ def tile_representationngramestimator_kernel(tc, table, w, b, offs, out):
                         stop=(slot == SLOTS - 1),
                     )
                 biased = staging.tile([P, PIECE], F32, name="biased")
-                nc.vector.tensor_scalar(
-                    biased[:], scores[:], biases[block][:, 0:1], None, mybir.AluOpType.add
-                )
+                if piece % 2 == 0:
+                    nc.vector.tensor_scalar(
+                        biased[:], scores[:], biases[block][:, 0:1], None, mybir.AluOpType.add
+                    )
+                else:
+                    nc.scalar.activation(
+                        biased[:], scores[:], mybir.ActivationFunctionType.Identity, bias=biases[block][:, 0:1]
+                    )
                 nc.sync.dma_start(
                     out[block * P : (block + 1) * P, piece * PIECE : (piece + 1) * PIECE], biased[:]
                 )

@@ -4,7 +4,9 @@ BF16, F32, U16 = mybir.dt.bfloat16, mybir.dt.float32, mybir.dt.uint16
 
 P = 128
 SYMBOLS = 256
+BLOCKS = SYMBOLS // P
 SLOTS = 4
+PAIR = 2
 CONTEXTS = 256
 PIECE = 128
 PER_COLUMN = 16
@@ -23,39 +25,38 @@ def tile_representationngramestimator_kernel(tc, table, w, b, offs, out):
         nc.sync.dma_start(offsets[:], offs)
         embeddings = held.tile([P, SYMBOLS], BF16, name="embeddings")
         nc.scalar.dma_start(embeddings[:], table)
+        by_block = w.rearrange("d (slot block m) -> d slot block m", slot=SLOTS, block=BLOCKS)
         weights = []
-        for slot in range(SLOTS):
-            slot_weights = held.tile([P, SYMBOLS], BF16, name=f"weights{slot}")
-            queue = nc.sync if slot % 2 == 0 else nc.scalar
-            queue.dma_start(slot_weights[:], w[:, slot * SYMBOLS : (slot + 1) * SYMBOLS])
-            weights.append(slot_weights)
+        for block in range(BLOCKS):
+            pairs = []
+            for pair in range(SLOTS // PAIR):
+                pair_weights = held.tile([P, PAIR, P], BF16, name=f"weights{block}{pair}")
+                queue = nc.sync if pair == 0 else nc.scalar
+                queue.dma_start(pair_weights[:], by_block[:, pair * PAIR : (pair + 1) * PAIR, block, :])
+                pairs.append(pair_weights)
+            weights.append(pairs)
         biases = []
-        for block in range(SYMBOLS // P):
+        for block in range(BLOCKS):
             bias = held.tile([P, 1], F32, name=f"bias{block}")
             nc.scalar.dma_start(bias[:], b[block * P : (block + 1) * P, :])
             biases.append(bias)
 
-        for block in range(SYMBOLS // P):
+        for block in range(BLOCKS):
             for piece in range(CONTEXTS // PIECE):
                 scores = psum.tile([P, PIECE], F32, name="scores")
                 for slot in range(SLOTS):
                     first = (slot * CONTEXTS + piece * PIECE) // PER_COLUMN
                     nc.tensor.matmul(
                         scores[:],
-                        weights[slot][:, block * P : (block + 1) * P],
+                        weights[block][slot // PAIR][:, slot % PAIR, :],
                         embeddings[:].indirect(offsets[:, first : first + PIECE // PER_COLUMN]),
                         start=(slot == 0),
                         stop=(slot == SLOTS - 1),
                     )
                 biased = staging.tile([P, PIECE], F32, name="biased")
-                if piece % 2 == 0:
-                    nc.vector.tensor_scalar(
-                        biased[:], scores[:], biases[block][:, 0:1], None, mybir.AluOpType.add
-                    )
-                else:
-                    nc.scalar.activation(
-                        biased[:], scores[:], mybir.ActivationFunctionType.Identity, bias=biases[block][:, 0:1]
-                    )
+                nc.vector.tensor_scalar(
+                    biased[:], scores[:], biases[block][:, 0:1], None, mybir.AluOpType.add
+                )
                 nc.sync.dma_start(
                     out[block * P : (block + 1) * P, piece * PIECE : (piece + 1) * PIECE], biased[:]
                 )

@@ -6,7 +6,7 @@ P = 128
 SYMBOLS = 256
 BLOCKS = SYMBOLS // P
 SLOTS = 4
-PAIR = 2
+EARLY_SLOTS = 2
 CONTEXTS = 256
 PIECE = 128
 PER_COLUMN = 16
@@ -16,47 +16,51 @@ FLOPS = 2 * P * SLOTS * SYMBOLS * CONTEXTS
 
 def tile_representationngramestimator_kernel(tc, table, w, b, offs, out):
     nc = tc.nc
+    groups = [(block, piece) for block in range(BLOCKS) for piece in range(CONTEXTS // PIECE)]
     with (
         tc.tile_pool(name="held", bufs=1) as held,
-        tc.tile_pool(name="staging", bufs=4) as staging,
-        tc.psum_pool(name="psum", bufs=4) as psum,
+        tc.tile_pool(name="staging", bufs=len(groups)) as staging,
+        tc.psum_pool(name="psum", bufs=1) as psum,
     ):
         offsets = held.tile([P, SLOTS * CONTEXTS // PER_COLUMN], U16, name="offsets")
         nc.sync.dma_start(offsets[:], offs)
         embeddings = held.tile([P, SYMBOLS], BF16, name="embeddings")
         nc.scalar.dma_start(embeddings[:], table)
-        by_block = w.rearrange("d (slot block m) -> d slot block m", slot=SLOTS, block=BLOCKS)
         weights = []
-        for block in range(BLOCKS):
-            pairs = []
-            for pair in range(SLOTS // PAIR):
-                pair_weights = held.tile([P, PAIR, P], BF16, name=f"weights{block}{pair}")
-                queue = nc.sync if pair == 0 else nc.scalar
-                queue.dma_start(pair_weights[:], by_block[:, pair * PAIR : (pair + 1) * PAIR, block, :])
-                pairs.append(pair_weights)
-            weights.append(pairs)
+        for slot in range(SLOTS):
+            slot_weights = held.tile([P, SYMBOLS], BF16, name=f"weights{slot}")
+            queue = nc.sync if slot % 2 == 0 else nc.scalar
+            queue.dma_start(slot_weights[:], w[:, slot * SYMBOLS : (slot + 1) * SYMBOLS])
+            weights.append(slot_weights)
         biases = []
         for block in range(BLOCKS):
             bias = held.tile([P, 1], F32, name=f"bias{block}")
             nc.scalar.dma_start(bias[:], b[block * P : (block + 1) * P, :])
             biases.append(bias)
 
-        for block in range(BLOCKS):
-            for piece in range(CONTEXTS // PIECE):
-                scores = psum.tile([P, PIECE], F32, name="scores")
-                for slot in range(SLOTS):
-                    first = (slot * CONTEXTS + piece * PIECE) // PER_COLUMN
-                    nc.tensor.matmul(
-                        scores[:],
-                        weights[block][slot // PAIR][:, slot % PAIR, :],
-                        embeddings[:].indirect(offsets[:, first : first + PIECE // PER_COLUMN]),
-                        start=(slot == 0),
-                        stop=(slot == SLOTS - 1),
-                    )
-                biased = staging.tile([P, PIECE], F32, name="biased")
-                nc.vector.tensor_scalar(
-                    biased[:], scores[:], biases[block][:, 0:1], None, mybir.AluOpType.add
-                )
-                nc.sync.dma_start(
-                    out[block * P : (block + 1) * P, piece * PIECE : (piece + 1) * PIECE], biased[:]
-                )
+        scores = [psum.tile([P, PIECE], F32, name=f"scores{g}") for g in range(len(groups))]
+
+        def project(slot, g):
+            block, piece = groups[g]
+            first = (slot * CONTEXTS + piece * PIECE) // PER_COLUMN
+            nc.tensor.matmul(
+                scores[g][:],
+                weights[slot][:, block * P : (block + 1) * P],
+                embeddings[:].indirect(offsets[:, first : first + PIECE // PER_COLUMN]),
+                start=(slot == 0),
+                stop=(slot == SLOTS - 1),
+            )
+
+        for slot in range(EARLY_SLOTS):
+            for g in range(len(groups)):
+                project(slot, g)
+        for g, (block, piece) in enumerate(groups):
+            for slot in range(EARLY_SLOTS, SLOTS):
+                project(slot, g)
+            biased = staging.tile([P, PIECE], F32, name="biased")
+            nc.vector.tensor_scalar(
+                biased[:], scores[g][:], biases[block][:, 0:1], None, mybir.AluOpType.add
+            )
+            nc.sync.dma_start(
+                out[block * P : (block + 1) * P, piece * PIECE : (piece + 1) * PIECE], biased[:]
+            )

@@ -35,7 +35,8 @@ def tile_representationngramestimator_kernel(tc, table, w, b, offs, out):
         biases = []
         for block in range(BLOCKS):
             bias = held.tile([P, 1], F32, name=f"bias{block}")
-            nc.scalar.dma_start(bias[:], b[block * P : (block + 1) * P, :])
+            queue = nc.sync if block % 2 == 0 else nc.scalar
+            queue.dma_start(bias[:], b[block * P : (block + 1) * P, :])
             biases.append(bias)
 
         scores = [psum.tile([P, PIECE], F32, name=f"scores{g}") for g in range(len(groups))]

@@ -3,6 +3,7 @@ import concourse.mybir as mybir
 BF16, F32, U16 = mybir.dt.bfloat16, mybir.dt.float32, mybir.dt.uint16
 
 P = 128
+HALF_P = P // 2
 SYMBOLS = 256
 BLOCKS = SYMBOLS // P
 SLOTS = 4
@@ -62,6 +63,10 @@ def tile_representationngramestimator_kernel(tc, table, w, b, offs, out):
             nc.vector.tensor_scalar(
                 biased[:], scores[g][:], biases[block][:, 0:1], None, mybir.AluOpType.add
             )
-            nc.sync.dma_start(
-                out[block * P : (block + 1) * P, piece * PIECE : (piece + 1) * PIECE], biased[:]
-            )
+            for half, queue in enumerate((nc.sync, nc.scalar)):
+                rows = slice(half * HALF_P, (half + 1) * HALF_P)
+                first_row = block * P + half * HALF_P
+                queue.dma_start(
+                    out[first_row : first_row + HALF_P, piece * PIECE : (piece + 1) * PIECE],
+                    biased[rows, :],
+                )

@@ -27,18 +27,17 @@ def tile_representationngramestimator_kernel(tc, table, w, b, offs, out):
         nc.sync.dma_start(offsets[:], offs)
         embeddings = held.tile([P, SYMBOLS], BF16, name="embeddings")
         nc.scalar.dma_start(embeddings[:], table)
-        weights = []
-        for slot in range(SLOTS):
-            slot_weights = held.tile([P, SYMBOLS], BF16, name=f"weights{slot}")
-            queue = nc.sync if slot % 2 == 0 else nc.scalar
-            queue.dma_start(slot_weights[:], w[:, slot * SYMBOLS : (slot + 1) * SYMBOLS])
-            weights.append(slot_weights)
-        biases = []
-        for block in range(BLOCKS):
-            bias = held.tile([P, 1], F32, name=f"bias{block}")
-            queue = nc.sync if block % 2 == 0 else nc.scalar
-            queue.dma_start(bias[:], b[block * P : (block + 1) * P, :])
-            biases.append(bias)
+        loads = [(0, block * P, P) for block in range(BLOCKS)]
+        loads += [(slot, 0, SYMBOLS) for slot in range(1, SLOTS)]
+        weights = {}
+        for i, (slot, first, columns) in enumerate(loads):
+            part = held.tile([P, columns], BF16, name=f"weights{slot}_{first}")
+            queue = nc.sync if i % 2 == 0 else nc.scalar
+            queue.dma_start(part[:], w[:, slot * SYMBOLS + first : slot * SYMBOLS + first + columns])
+            for block in range(first // P, (first + columns) // P):
+                weights[slot, block] = part[:, block * P - first : (block + 1) * P - first]
+        biases = held.tile([P, BLOCKS], F32, name="biases")
+        nc.scalar.dma_start(biases[:], b.rearrange("(a p) o -> p (a o)", p=P))
 
         scores = [psum.tile([P, PIECE], F32, name=f"scores{g}") for g in range(len(groups))]
 
@@ -47,7 +46,7 @@ def tile_representationngramestimator_kernel(tc, table, w, b, offs, out):
             first = (slot * CONTEXTS + piece * PIECE) // PER_COLUMN
             nc.tensor.matmul(
                 scores[g][:],
-                weights[slot][:, block * P : (block + 1) * P],
+                weights[slot, block],
                 embeddings[:].indirect(offsets[:, first : first + PIECE // PER_COLUMN]),
                 start=(slot == 0),
                 stop=(slot == SLOTS - 1),
@@ -61,7 +60,7 @@ def tile_representationngramestimator_kernel(tc, table, w, b, offs, out):
                 project(slot, g)
             biased = staging.tile([P, PIECE], F32, name="biased")
             nc.vector.tensor_scalar(
-                biased[:], scores[g][:], biases[block][:, 0:1], None, mybir.AluOpType.add
+                biased[:], scores[g][:], biases[:, block : block + 1], None, mybir.AluOpType.add
             )
             for half, queue in enumerate((nc.sync, nc.scalar)):
                 rows = slice(half * HALF_P, (half + 1) * HALF_P)

@@ -27,15 +27,21 @@ def tile_representationngramestimator_kernel(tc, table, w, b, offs, out):
         nc.sync.dma_start(offsets[:], offs)
         embeddings = held.tile([P, SYMBOLS], BF16, name="embeddings")
         nc.scalar.dma_start(embeddings[:], table)
-        loads = [(0, block * P, P) for block in range(BLOCKS)]
-        loads += [(slot, 0, SYMBOLS) for slot in range(1, SLOTS)]
+        w_slots = w.rearrange("d (k m) -> d k m", k=SLOTS)
         weights = {}
-        for i, (slot, first, columns) in enumerate(loads):
-            part = held.tile([P, columns], BF16, name=f"weights{slot}_{first}")
-            queue = nc.sync if i % 2 == 0 else nc.scalar
-            queue.dma_start(part[:], w[:, slot * SYMBOLS + first : slot * SYMBOLS + first + columns])
-            for block in range(first // P, (first + columns) // P):
-                weights[slot, block] = part[:, block * P - first : (block + 1) * P - first]
+        for queue, slots, blocks in (
+            (nc.sync, range(1), range(1)),
+            (nc.scalar, range(1), range(1, BLOCKS)),
+            (nc.sync, range(1, EARLY_SLOTS), range(BLOCKS)),
+            (nc.scalar, range(EARLY_SLOTS, SLOTS), range(1)),
+            (nc.sync, range(EARLY_SLOTS, SLOTS), range(1, BLOCKS)),
+        ):
+            columns = slice(blocks.start * P, blocks.stop * P)
+            part = held.tile([P, len(slots), len(blocks) * P], BF16, name=f"weights{slots.start}_{blocks.start}")
+            queue.dma_start(part[:], w_slots[:, slots.start : slots.stop, columns])
+            for i, slot in enumerate(slots):
+                for j, block in enumerate(blocks):
+                    weights[slot, block] = part[:, i, j * P : (j + 1) * P]
         biases = held.tile([P, BLOCKS], F32, name="biases")
         nc.scalar.dma_start(biases[:], b.rearrange("(a p) o -> p (a o)", p=P))
 

import concourse.mybir as mybir

BF16, F32, U16 = mybir.dt.bfloat16, mybir.dt.float32, mybir.dt.uint16

P = 128
HALF_P = P // 2
SYMBOLS = 256
BLOCKS = SYMBOLS // P
SLOTS = 4
EARLY_SLOTS = 2
CONTEXTS = 256
PIECE = 128
PER_COLUMN = 16

FLOPS = 2 * P * SLOTS * SYMBOLS * CONTEXTS


def tile_representationngramestimator_kernel(tc, table, w, b, offs, out):
    nc = tc.nc
    groups = [(block, piece) for block in range(BLOCKS) for piece in range(CONTEXTS // PIECE)]
    with (
        tc.tile_pool(name="held", bufs=1) as held,
        tc.tile_pool(name="staging", bufs=len(groups)) as staging,
        tc.psum_pool(name="psum", bufs=1) as psum,
    ):
        offsets = held.tile([P, SLOTS * CONTEXTS // PER_COLUMN], U16, name="offsets")
        nc.sync.dma_start(offsets[:], offs)
        embeddings = held.tile([P, SYMBOLS], BF16, name="embeddings")
        nc.scalar.dma_start(embeddings[:], table)
        w_slots = w.rearrange("d (k m) -> d k m", k=SLOTS)
        weights = {}
        for queue, slots, blocks in (
            (nc.sync, range(1), range(1)),
            (nc.scalar, range(1), range(1, BLOCKS)),
            (nc.sync, range(1, EARLY_SLOTS), range(BLOCKS)),
            (nc.scalar, range(EARLY_SLOTS, SLOTS), range(1)),
            (nc.sync, range(EARLY_SLOTS, SLOTS), range(1, BLOCKS)),
        ):
            columns = slice(blocks.start * P, blocks.stop * P)
            part = held.tile([P, len(slots), len(blocks) * P], BF16, name=f"weights{slots.start}_{blocks.start}")
            queue.dma_start(part[:], w_slots[:, slots.start : slots.stop, columns])
            for i, slot in enumerate(slots):
                for j, block in enumerate(blocks):
                    weights[slot, block] = part[:, i, j * P : (j + 1) * P]
        biases = held.tile([P, BLOCKS], F32, name="biases")
        nc.scalar.dma_start(biases[:], b.rearrange("(a p) o -> p (a o)", p=P))

        scores = [psum.tile([P, PIECE], F32, name=f"scores{g}") for g in range(len(groups))]

        def project(slot, g):
            block, piece = groups[g]
            first = (slot * CONTEXTS + piece * PIECE) // PER_COLUMN
            nc.tensor.matmul(
                scores[g][:],
                weights[slot, block],
                embeddings[:].indirect(offsets[:, first : first + PIECE // PER_COLUMN]),
                start=(slot == 0),
                stop=(slot == SLOTS - 1),
            )

        for slot in range(EARLY_SLOTS):
            for g in range(len(groups)):
                project(slot, g)
        for g, (block, piece) in enumerate(groups):
            for slot in range(EARLY_SLOTS, SLOTS):
                project(slot, g)
            biased = staging.tile([P, PIECE], F32, name="biased")
            nc.vector.tensor_scalar(
                biased[:], scores[g][:], biases[:, block : block + 1], None, mybir.AluOpType.add
            )
            for half, queue in enumerate((nc.sync, nc.scalar)):
                rows = slice(half * HALF_P, (half + 1) * HALF_P)
                first_row = block * P + half * HALF_P
                queue.dma_start(
                    out[first_row : first_row + HALF_P, piece * PIECE : (piece + 1) * PIECE],
                    biased[rows, :],
                )
